import numpy as np
import ml_dtypes


def mxq(x, axis, fmt="e4m3"):
    dtype, down = {"e4m3": (ml_dtypes.float8_e4m3fn, 7), "e5m2": (ml_dtypes.float8_e5m2, 14)}[fmt]
    v = np.moveaxis(np.asarray(x, np.float32).astype(ml_dtypes.bfloat16).astype(np.float64), axis, -1)
    blocks = v.reshape(v.shape[:-1] + (-1, 32))
    amax = np.abs(blocks).max(-1, keepdims=True)
    byte = np.maximum(np.where(amax > 0, np.frexp(amax)[1] - 1 + 127, 0) - down, 1)
    scale = np.exp2(byte - 127.0)
    codes = (blocks / scale).astype(np.float32).astype(dtype).astype(np.float64)
    return np.moveaxis((codes * scale).reshape(v.shape), -1, axis)


WIDE = False


def mx_kscale(k):
    if not WIDE:
        return np.ones(k)
    levels = np.array([10, -10, 5, -5, 0])
    if k % 512:
        return np.exp2(np.random.permutation(np.resize(levels, k // 32))).repeat(32)
    a = np.empty((k // 512, 16))
    for p in range(k // 512):
        a[p, :8] = np.random.permutation(np.resize(levels, 8))
        for g in range(8):
            far = levels[np.abs(levels - a[p, g]) >= 10]
            a[p, g + 8] = far[np.random.randint(len(far))]
    return np.exp2(a.ravel()).repeat(32)


BF16 = ml_dtypes.bfloat16


def bf(x):
    return np.asarray(x, np.float32).astype(BF16)


def f64(x):
    return np.asarray(x).astype(np.float64)


B, Q, D = 256, 2048, 512
COMBOS = ((0, 1), (0, 2), (0, 3), (1, 0), (1, 2), (2, 0), (2, 1), (3, 0))
T = 0.07
V = 1 + max(max(c) for c in COMBOS)


def setup_inputs():
    s = mx_kscale(D)
    c = np.mean(s * s)
    shared = np.random.standard_normal((B, D))
    d = {}
    for v in range(V):
        gain = np.random.uniform(0.6, 1.6, (B, 1))
        own = np.random.standard_normal((B, D))
        d["x%d" % v] = bf((np.sqrt(0.1) * shared + np.sqrt(0.9) * own) * gain * s)
    for v in range(V):
        d["mem%d" % v] = bf(np.random.standard_normal((Q, D)) * c / s)
    return d


def core(x0, x1, x2, x3, mem0, mem1, mem2, mem3):
    X = [f64(x0), f64(x1), f64(x2), f64(x3)]
    Mem = [f64(mem0), f64(mem1), f64(mem2), f64(mem3)]
    Xn = [np.sqrt(np.sum(x * x, axis=1, keepdims=True)) for x in X]
    Xq = [mxq(x, 1, "e4m3") for x in X]
    Mq = [mxq(m, 1, "e4m3") for m in Mem]
    outs = []
    for i, j in COMBOS:
        self_dot = np.sum(X[i] * X[j], axis=1, keepdims=True)
        mem_dot = Xq[i] @ Mq[j].T
        logits = np.concatenate([self_dot, mem_dot], axis=1)
        outs.append(np.exp(logits / (Xn[i] * Xn[j]) / T))
    return np.stack(outs)


def e4m3fn_bytes(y):
    return np.clip(np.asarray(y, np.float64), -448.0, 448.0).astype(np.float32).astype(ml_dtypes.float8_e4m3fn).view(np.uint8)


Y_SCALE = 140.0


def reference(x0, x1, x2, x3, mem0, mem1, mem2, mem3):
    out = core(x0, x1, x2, x3, mem0, mem1, mem2, mem3)
    return out, e4m3fn_bytes(out * Y_SCALE)

@@ -1,0 +1,210 @@
+from contextlib import ExitStack
+
+import concourse.mybir as mybir
+from concourse.masks import make_identity
+
+F32 = mybir.dt.float32
+BF16 = mybir.dt.bfloat16
+U32 = mybir.dt.uint32
+U8 = mybir.dt.uint8
+FP8X4 = mybir.dt.float8_e4m3fn_x4
+FP8 = mybir.dt.float8_e4m3fn
+ACT = mybir.ActivationFunctionType
+ALU = mybir.AluOpType
+
+B, Q, D = 256, 2048, 512
+COMBOS = ((0, 1), (0, 2), (0, 3), (1, 0), (1, 2), (2, 0), (2, 1), (3, 0))
+PAIRS = ((0, 1), (0, 2), (0, 3), (1, 2))
+TEMP = 0.07
+Y_SCALE = 140.0
+FLOPS = 2 * len(COMBOS) * B * Q * D
+
+P = 128
+W = Q + 1
+NCH = 4
+ORDER = (3, 5, 7, 0, 6, 1, 4, 2)
+
+
+def tile_memorymoco_pa_kernel(tc, x0, x1, x2, x3, mem0, mem1, mem2, mem3, out_0, out_1):
+    nc = tc.nc
+    xs = (x0, x1, x2, x3)
+    mems = (mem0, mem1, mem2, mem3)
+
+    with ExitStack() as ctx:
+        const = ctx.enter_context(tc.tile_pool(name="const", bufs=1))
+        rawp = ctx.enter_context(tc.tile_pool(name="rawp", bufs=12))
+        grp = ctx.enter_context(tc.tile_pool(name="grp", bufs=3))
+        outp = ctx.enter_context(tc.tile_pool(name="outp", bufs=4))
+        ptp = ctx.enter_context(tc.psum_pool(name="ptp", bufs=3))
+        psp = ctx.enter_context(tc.psum_pool(name="psp", bufs=5))
+
+        ident = const.tile([P, P], F32, name="ident")
+        make_identity(nc, ident[:])
+        one = const.tile([P, 1], F32, name="one")
+        nc.vector.memset(one[:], 1.0)
+        warm = const.tile([P, 2], F32, name="warm")
+        nc.scalar.activation(out=warm[:, 0:1], in_=one[:], func=ACT.Sqrt)
+
+        xr = {}
+        for v in (1, 0, 2, 3):
+            xr[v] = const.tile([P, 2, D], BF16, name="xr%d" % v)
+            nc.sync.dma_start(out=xr[v][:], in_=xs[v].rearrange("(p m) k -> p m k", m=2))
+        raw = {}
+        for j in range(4):
+            for n in range(NCH):
+                raw[(j, n)] = rawp.tile([P, 4, D], BF16, name="raw%d_%d" % (j, n), tag="raw")
+                nc.sync.dma_start(
+                    out=raw[(j, n)][:],
+                    in_=mems[j][512 * n : 512 * (n + 1), :].rearrange("(p r) k -> p r k", r=4),
+                )
+
+        ss = const.tile([P, 8], F32, name="ss")
+        nrm = const.tile([P, 8], F32, name="nrm")
+        junk_s = const.tile([P, D], BF16, name="junk_s")
+        junk_v = const.tile([P, D], BF16, name="junk_v")
+        for v in (1, 0, 2, 3):
+            for m in range(2):
+                nc.scalar.activation(
+                    out=junk_s[:], in_=xr[v][:, m, :], func=ACT.Square,
+                    accum_out=ss[:, 2 * v + m : 2 * v + m + 1],
+                )
+        nc.scalar.activation(out=nrm[:], in_=ss[:], func=ACT.Sqrt)
+        nc.scalar.activation(out=warm[:, 1:2], in_=nrm[:, 0:1], func=ACT.Exp, scale=0.0)
+
+        prod = const.tile([P, 4, 2], F32, name="prod")
+        rs = const.tile([P, 4, 2], F32, name="rs")
+        dots = const.tile([P, 4, 2], F32, name="dots")
+        lg0 = const.tile([P, 4, 2, 1], F32, name="lg0")
+        for k in range(4):
+            i, j = PAIRS[k]
+            nc.vector.scalar_tensor_tensor(
+                out=prod[:, k, :], in0=nrm[:, 2 * i : 2 * i + 2], scalar=TEMP,
+                in1=nrm[:, 2 * j : 2 * j + 2], op0=ALU.mult, op1=ALU.mult,
+            )
+        nc.vector.reciprocal(out=rs[:], in_=prod[:])
+
+        xc = {}
+        xsc = {}
+        mc = {}
+        msc = {}
+        for v in range(4):
+            xc[v] = const.tile([P, 2 * P], U32, name="xc%d" % v, align_bytes=64)
+            xsc[v] = const.tile([P, 2 * P], U8, name="xsc%d" % v, align_bytes=64)
+            mc[v] = const.tile([P, Q], U32, name="mc%d" % v, align_bytes=64)
+            msc[v] = const.tile([P, Q], U8, name="msc%d" % v, align_bytes=64)
+
+        def prep_x(v):
+            words = xr[v][:].bitcast(F32)
+            pt = ptp.tile([P, 2, 2, P], F32, name="ptx%d" % v, tag="pt")
+            for m in range(2):
+                for u in range(2):
+                    nc.tensor.transpose(pt[:, m, u, :], words[:, m, u : D // 2 : 2], ident[:])
+            gx = grp.tile([P, 8 * P], BF16, name="gx%d" % v, tag="gx", align_bytes=64)
+            nc.vector.tensor_copy(
+                out=gx[:].bitcast(F32).rearrange("k (m q u) -> k m q u", m=2, u=2),
+                in_=pt[:].rearrange("k m u q -> k m q u"),
+            )
+            nc.vector.quantize_mx(out=xc[v][:].bitcast(FP8X4), scales=xsc[v][:], in_=gx[:])
+
+        def prep(j, n):
+            t = 4 * j + n
+            words = raw[(j, n)][:].bitcast(F32)
+            g = grp.tile([P, 4 * 512], BF16, name="g%d" % t, tag="g", align_bytes=64)
+            gw = g[:].bitcast(F32).rearrange("k (h r q u) -> k h r q u", h=2, r=2, u=2)
+            for h in range(2):
+                pt = ptp.tile([P, 2, 2, P], F32, name="pt%d_%d" % (t, h), tag="pt")
+                for r in range(2):
+                    for u in range(2):
+                        nc.tensor.transpose(pt[:, r, u, :], words[:, 2 * h + r, u : D // 2 : 2], ident[:])
+                src = pt[:].rearrange("k r u q -> k r q u")
+                if h == 1 and (t < 4 or t % 2 == 0):
+                    nc.scalar.copy(out=gw[:, h], in_=src)
+                else:
+                    nc.vector.tensor_copy(out=gw[:, h], in_=src)
+            cols = slice(512 * n, 512 * (n + 1))
+            nc.vector.quantize_mx(out=mc[j][:, cols].bitcast(FP8X4), scales=msc[j][:, cols], in_=g[:])
+
+        have_pair = set()
+        tiles = {}
+
+        def start_tile(c):
+            i, j = COMBOS[c]
+            k = PAIRS.index((min(i, j), max(i, j)))
+            if k not in have_pair:
+                have_pair.add(k)
+                a, b = PAIRS[k]
+                for m in range(2):
+                    nc.vector.scalar_tensor_tensor(
+                        out=junk_v[:], in0=xr[a][:, m, :], scalar=1.0, in1=xr[b][:, m, :],
+                        op0=ALU.mult, op1=ALU.mult, accum_out=dots[:, k, m : m + 1],
+                    )
+                nc.vector.tensor_tensor(
+                    out=lg0[:, k, :, 0], in0=dots[:, k, :], in1=rs[:, k, :], op=ALU.mult
+                )
+            ot = outp.tile([P, 2, W], F32, name="ot%d" % c, tag="ot")
+            o8 = outp.tile([P, 2, W], FP8, name="o8%d" % c, tag="o8")
+            nc.scalar.activation(out=ot[:, :, 0:1], in_=lg0[:, k], func=ACT.Exp)
+            tiles[c] = (ot, o8, k)
+
+        def mm(c, m, n):
+            i, j = COMBOS[c]
+            ot, o8, k = tiles[c]
+            ps = psp.tile([P, 512], F32, name="ps%d_%d_%d" % (c, m, n), tag="ps")
+            rows = slice(P * m, P * (m + 1))
+            cols = slice(512 * n, 512 * (n + 1))
+            nc.tensor.matmul_mx(
+                out=ps[:],
+                lhsT=xc[i][:, rows].bitcast(FP8X4), lhsT_scale=xsc[i][:, rows],
+                rhs=mc[j][:, cols].bitcast(FP8X4), rhs_scale=msc[j][:, cols],
+                start=True, stop=True,
+            )
+            nc.scalar.activation(
+                out=ot[:, m, 1 + 512 * n : 1 + 512 * (n + 1)].rearrange("b (q r) -> b q r", r=4),
+                in_=ps[:].rearrange("b (r q) -> b q r", r=4),
+                func=ACT.Exp, scale=rs[:, k, m : m + 1],
+            )
+
+        def finish_row(c, m):
+            ot, o8, k = tiles[c]
+            nc.vector.tensor_scalar(
+                out=o8[:, m, :], in0=ot[:, m, :], scalar1=Y_SCALE, scalar2=None,
+                op0=ALU.mult, saturate=False,
+            )
+            nc.sync.dma_start(
+                out=out_1[c].rearrange("(p m) q -> p m q", m=2)[:, m, :],
+                in_=o8[:, m, :].bitcast(U8),
+            )
+
+        def store_tile(c):
+            ot, o8, k = tiles[c]
+            nc.sync.dma_start(
+                out=out_0[c].rearrange("(p m) q -> p (m q)", m=2),
+                in_=ot[:].rearrange("p m q -> p (m q)"),
+            )
+
+        for v in (1, 2, 3):
+            prep_x(v)
+        prep(0, 0)
+        c = ORDER[0]
+        start_tile(c)
+        for n in range(NCH):
+            if n + 1 < NCH:
+                prep(0, n + 1)
+            mm(c, 0, n)
+            mm(c, 1, n)
+        store_tile(c)
+        finish_row(c, 0)
+        finish_row(c, 1)
+        prep_x(0)
+
+        nxt = 4
+        for c in ORDER[1:]:
+            start_tile(c)
+            for m in range(2):
+                if nxt < 16:
+                    prep(nxt // 4, nxt % 4)
+                    nxt += 1
+                for n in range(NCH):
+                    mm(c, m, n)
+                finish_row(c, m)
+            store_tile(c)

@@ -50,13 +50,13 @@ def tile_memorymoco_pa_kernel(tc, x0, x1, x2, x3, mem0, mem1, mem2, mem3, out_0,
             xr[v] = const.tile([P, 2, D], BF16, name="xr%d" % v)
             nc.sync.dma_start(out=xr[v][:], in_=xs[v].rearrange("(p m) k -> p m k", m=2))
         raw = {}
-        for j in range(4):
-            for n in range(NCH):
-                raw[(j, n)] = rawp.tile([P, 4, D], BF16, name="raw%d_%d" % (j, n), tag="raw")
-                nc.sync.dma_start(
-                    out=raw[(j, n)][:],
-                    in_=mems[j][512 * n : 512 * (n + 1), :].rearrange("(p r) k -> p r k", r=4),
-                )
+        for t in range(16):
+            raw[t] = rawp.tile([P, 4, D], BF16, name="raw%d" % t, tag="raw")
+            n = t % 4
+            nc.sync.dma_start(
+                out=raw[t][:],
+                in_=mems[t // 4][512 * n : 512 * (n + 1), :].rearrange("(p r) k -> p r k", r=4),
+            )
 
         ss = const.tile([P, 8], F32, name="ss")
         nrm = const.tile([P, 8], F32, name="nrm")
@@ -75,13 +75,6 @@ def tile_memorymoco_pa_kernel(tc, x0, x1, x2, x3, mem0, mem1, mem2, mem3, out_0,
         rs = const.tile([P, 4, 2], F32, name="rs")
         dots = const.tile([P, 4, 2], F32, name="dots")
         lg0 = const.tile([P, 4, 2, 1], F32, name="lg0")
-        for k in range(4):
-            i, j = PAIRS[k]
-            nc.vector.scalar_tensor_tensor(
-                out=prod[:, k, :], in0=nrm[:, 2 * i : 2 * i + 2], scalar=TEMP,
-                in1=nrm[:, 2 * j : 2 * j + 2], op0=ALU.mult, op1=ALU.mult,
-            )
-        nc.vector.reciprocal(out=rs[:], in_=prod[:])
 
         xc = {}
         xsc = {}
@@ -93,58 +86,76 @@ def tile_memorymoco_pa_kernel(tc, x0, x1, x2, x3, mem0, mem1, mem2, mem3, out_0,
             mc[v] = const.tile([P, Q], U32, name="mc%d" % v, align_bytes=64)
             msc[v] = const.tile([P, Q], U8, name="msc%d" % v, align_bytes=64)
 
-        def prep_x(v):
+        gxs = {}
+        gs = {}
+        tiles = {}
+
+        def scales():
+            for k in range(4):
+                i, j = PAIRS[k]
+                nc.vector.scalar_tensor_tensor(
+                    out=prod[:, k, :], in0=nrm[:, 2 * i : 2 * i + 2], scalar=TEMP,
+                    in1=nrm[:, 2 * j : 2 * j + 2], op0=ALU.mult, op1=ALU.mult,
+                )
+            nc.vector.reciprocal(out=rs[:], in_=prod[:])
+
+        def dot(k, m):
+            a, b = PAIRS[k]
+            nc.vector.scalar_tensor_tensor(
+                out=junk_v[:], in0=xr[a][:, m, :], scalar=1.0, in1=xr[b][:, m, :],
+                op0=ALU.mult, op1=ALU.mult, accum_out=dots[:, k, m : m + 1],
+            )
+            if m == 1:
+                nc.vector.tensor_tensor(
+                    out=lg0[:, k, :, 0], in0=dots[:, k, :], in1=rs[:, k, :], op=ALU.mult
+                )
+
+        def x_turn(v):
             words = xr[v][:].bitcast(F32)
             pt = ptp.tile([P, 2, 2, P], F32, name="ptx%d" % v, tag="pt")
             for m in range(2):
                 for u in range(2):
                     nc.tensor.transpose(pt[:, m, u, :], words[:, m, u : D // 2 : 2], ident[:])
-            gx = grp.tile([P, 8 * P], BF16, name="gx%d" % v, tag="gx", align_bytes=64)
+            gxs[v] = grp.tile([P, 8 * P], BF16, name="gx%d" % v, tag="gx", align_bytes=64)
             nc.vector.tensor_copy(
-                out=gx[:].bitcast(F32).rearrange("k (m q u) -> k m q u", m=2, u=2),
+                out=gxs[v][:].bitcast(F32).rearrange("k (m q u) -> k m q u", m=2, u=2),
                 in_=pt[:].rearrange("k m u q -> k m q u"),
             )
-            nc.vector.quantize_mx(out=xc[v][:].bitcast(FP8X4), scales=xsc[v][:], in_=gx[:])
 
-        def prep(j, n):
-            t = 4 * j + n
-            words = raw[(j, n)][:].bitcast(F32)
-            g = grp.tile([P, 4 * 512], BF16, name="g%d" % t, tag="g", align_bytes=64)
-            gw = g[:].bitcast(F32).rearrange("k (h r q u) -> k h r q u", h=2, r=2, u=2)
+        def x_quant(v):
+            nc.vector.quantize_mx(out=xc[v][:].bitcast(FP8X4), scales=xsc[v][:], in_=gxs[v][:])
+
+        def turn(t, on_scalar):
+            words = raw[t][:].bitcast(F32)
+            gs[t] = grp.tile([P, 4 * 512], BF16, name="g%d" % t, tag="g", align_bytes=64)
+            gw = gs[t][:].bitcast(F32).rearrange("k (h r q u) -> k h r q u", h=2, r=2, u=2)
             for h in range(2):
                 pt = ptp.tile([P, 2, 2, P], F32, name="pt%d_%d" % (t, h), tag="pt")
                 for r in range(2):
                     for u in range(2):
                         nc.tensor.transpose(pt[:, r, u, :], words[:, 2 * h + r, u : D // 2 : 2], ident[:])
                 src = pt[:].rearrange("k r u q -> k r q u")
-                if h == 1 and (t < 4 or t % 2 == 0):
+                if h == 1 and on_scalar:
                     nc.scalar.copy(out=gw[:, h], in_=src)
                 else:
                     nc.vector.tensor_copy(out=gw[:, h], in_=src)
-            cols = slice(512 * n, 512 * (n + 1))
-            nc.vector.quantize_mx(out=mc[j][:, cols].bitcast(FP8X4), scales=msc[j][:, cols], in_=g[:])
 
-        have_pair = set()
-        tiles = {}
+        def quant(t):
+            cols = slice(512 * (t % 4), 512 * (t % 4 + 1))
+            nc.vector.quantize_mx(
+                out=mc[t // 4][:, cols].bitcast(FP8X4), scales=msc[t // 4][:, cols], in_=gs[t][:]
+            )
 
         def start_tile(c):
             i, j = COMBOS[c]
             k = PAIRS.index((min(i, j), max(i, j)))
-            if k not in have_pair:
-                have_pair.add(k)
-                a, b = PAIRS[k]
-                for m in range(2):
-                    nc.vector.scalar_tensor_tensor(
-                        out=junk_v[:], in0=xr[a][:, m, :], scalar=1.0, in1=xr[b][:, m, :],
-                        op0=ALU.mult, op1=ALU.mult, accum_out=dots[:, k, m : m + 1],
-                    )
-                nc.vector.tensor_tensor(
-                    out=lg0[:, k, :, 0], in0=dots[:, k, :], in1=rs[:, k, :], op=ALU.mult
-                )
             ot = outp.tile([P, 2, W], F32, name="ot%d" % c, tag="ot")
             o8 = outp.tile([P, 2, W], FP8, name="o8%d" % c, tag="o8")
-            nc.scalar.activation(out=ot[:, :, 0:1], in_=lg0[:, k], func=ACT.Exp)
             tiles[c] = (ot, o8, k)
+
+        def col0(c):
+            ot, o8, k = tiles[c]
+            nc.scalar.activation(out=ot[:, :, 0:1], in_=lg0[:, k], func=ACT.Exp)
 
         def mm(c, m, n):
             i, j = COMBOS[c]
@@ -164,47 +175,77 @@ def tile_memorymoco_pa_kernel(tc, x0, x1, x2, x3, mem0, mem1, mem2, mem3, out_0,
                 func=ACT.Exp, scale=rs[:, k, m : m + 1],
             )
 
-        def finish_row(c, m):
+        def store32(c, m, lo, hi):
+            ot, o8, k = tiles[c]
+            nc.sync.dma_start(
+                out=out_0[c].rearrange("(p m) q -> p m q", m=2)[:, m, lo:hi], in_=ot[:, m, lo:hi]
+            )
+
+        def cast8(c, m, lo, hi):
             ot, o8, k = tiles[c]
             nc.vector.tensor_scalar(
-                out=o8[:, m, :], in0=ot[:, m, :], scalar1=Y_SCALE, scalar2=None,
+                out=o8[:, m, lo:hi], in0=ot[:, m, lo:hi], scalar1=Y_SCALE, scalar2=None,
                 op0=ALU.mult, saturate=False,
             )
             nc.sync.dma_start(
-                out=out_1[c].rearrange("(p m) q -> p m q", m=2)[:, m, :],
-                in_=o8[:, m, :].bitcast(U8),
+                out=out_1[c].rearrange("(p m) q -> p m q", m=2)[:, m, lo:hi],
+                in_=o8[:, m, lo:hi].bitcast(U8),
             )
 
-        def store_tile(c):
-            ot, o8, k = tiles[c]
-            nc.sync.dma_start(
-                out=out_0[c].rearrange("(p m) q -> p (m q)", m=2),
-                in_=ot[:].rearrange("p m q -> p (m q)"),
-            )
+        rows_seq = [(c, m) for c in ORDER for m in range(2)]
 
-        for v in (1, 2, 3):
-            prep_x(v)
-        prep(0, 0)
+        ctx.enter_context(tc.manual_schedule(engines={mybir.EngineType.DVE}))
+        x_turn(1)
+        x_turn(2)
+        x_quant(1)
+        x_turn(3)
+        x_quant(2)
+        x_quant(3)
+        turn(0, False)
+        scales()
+        quant(0)
         c = ORDER[0]
         start_tile(c)
+        seps = ((0, 0), (0, 1), (1, 0))
         for n in range(NCH):
-            if n + 1 < NCH:
-                prep(0, n + 1)
+            turn(n + 1, True)
             mm(c, 0, n)
             mm(c, 1, n)
-        store_tile(c)
-        finish_row(c, 0)
-        finish_row(c, 1)
-        prep_x(0)
-
-        nxt = 4
-        for c in ORDER[1:]:
-            start_tile(c)
-            for m in range(2):
-                if nxt < 16:
-                    prep(nxt // 4, nxt % 4)
-                    nxt += 1
+            if n < 3:
+                dot(seps[n][0], seps[n][1])
+                quant(n + 1)
+        col0(c)
+        store32(c, 0, 0, W)
+        store32(c, 1, 0, W)
+        dot(1, 1)
+        extras = {2: ("d", 2, 0), 3: ("d", 2, 1), 4: ("x", 0), 5: ("d", 3, 0), 6: ("d", 3, 1)}
+        for s in range(2, 16):
+            c, m = rows_seq[s]
+            if m == 0:
+                start_tile(c)
+                col0(c)
+            if s == 2:
+                cast8(rows_seq[0][0], 0, 0, W)
+            cast8(rows_seq[s - 1][0], rows_seq[s - 1][1], 0, W)
+            t = s + 3
+            if t < 16:
+                turn(t, t % 2 == 0)
+            e = extras.get(s)
+            if e is not None and e[0] == "x":
+                x_turn(0)
+            if e is not None and e[0] == "d":
+                dot(e[1], e[2])
+            if t - 1 < 16:
+                quant(t - 1)
+            if e is not None and e[0] == "x":
+                x_quant(0)
+            if s < 15:
                 for n in range(NCH):
                     mm(c, m, n)
-                finish_row(c, m)
-            store_tile(c)
+                store32(c, m, 0, W)
+            else:
+                for n in range(NCH):
+                    mm(c, m, n)
+                    lo = 0 if n == 0 else 1 + 512 * n
+                    store32(c, m, lo, 1 + 512 * (n + 1))
+                    cast8(c, m, lo, 1 + 512 * (n + 1))

@@ -32,9 +32,9 @@ def tile_memorymoco_pa_kernel(tc, x0, x1, x2, x3, mem0, mem1, mem2, mem3, out_0,
 
     with ExitStack() as ctx:
         const = ctx.enter_context(tc.tile_pool(name="const", bufs=1))
-        rawp = ctx.enter_context(tc.tile_pool(name="rawp", bufs=12))
         grp = ctx.enter_context(tc.tile_pool(name="grp", bufs=3))
-        outp = ctx.enter_context(tc.tile_pool(name="outp", bufs=4))
+        big = ctx.enter_context(tc.tile_pool(name="big", bufs=2))
+        outp = ctx.enter_context(tc.tile_pool(name="outp", bufs=3))
         ptp = ctx.enter_context(tc.psum_pool(name="ptp", bufs=3))
         psp = ctx.enter_context(tc.psum_pool(name="psp", bufs=5))
 
@@ -49,14 +49,17 @@ def tile_memorymoco_pa_kernel(tc, x0, x1, x2, x3, mem0, mem1, mem2, mem3, out_0,
         for v in (1, 0, 2, 3):
             xr[v] = const.tile([P, 2, D], BF16, name="xr%d" % v)
             nc.sync.dma_start(out=xr[v][:], in_=xs[v].rearrange("(p m) k -> p m k", m=2))
-        raw = {}
-        for t in range(16):
-            raw[t] = rawp.tile([P, 4, D], BF16, name="raw%d" % t, tag="raw")
-            n = t % 4
+        raw0 = {}
+        for n in range(NCH):
+            raw0[n] = const.tile([P, 4, D], BF16, name="raw0_%d" % n)
             nc.sync.dma_start(
-                out=raw[t][:],
-                in_=mems[t // 4][512 * n : 512 * (n + 1), :].rearrange("(p r) k -> p r k", r=4),
+                out=raw0[n][:],
+                in_=mem0[512 * n : 512 * (n + 1), :].rearrange("(p r) k -> p r k", r=4),
             )
+        rawj = {}
+        for j in (1, 2, 3):
+            rawj[j] = const.tile([P, 16, D], BF16, name="rawj%d" % j)
+            nc.sync.dma_start(out=rawj[j][:], in_=mems[j].rearrange("(p r) k -> p r k", r=16))
 
         ss = const.tile([P, 8], F32, name="ss")
         nrm = const.tile([P, 8], F32, name="nrm")
@@ -78,17 +81,19 @@ def tile_memorymoco_pa_kernel(tc, x0, x1, x2, x3, mem0, mem1, mem2, mem3, out_0,
 
         xc = {}
         xsc = {}
-        mc = {}
-        msc = {}
         for v in range(4):
             xc[v] = const.tile([P, 2 * P], U32, name="xc%d" % v, align_bytes=64)
             xsc[v] = const.tile([P, 2 * P], U8, name="xsc%d" % v, align_bytes=64)
-            mc[v] = const.tile([P, Q], U32, name="mc%d" % v, align_bytes=64)
-            msc[v] = const.tile([P, Q], U8, name="msc%d" % v, align_bytes=64)
-
+        mc = {}
+        msc = {}
         gxs = {}
         gs = {}
+        gbig = {}
         tiles = {}
+
+        def new_codes(j):
+            mc[j] = big.tile([P, Q], U32, name="mc%d" % j, tag="mc", align_bytes=64)
+            msc[j] = big.tile([P, Q], U8, name="msc%d" % j, tag="msc", align_bytes=64)
 
         def scales():
             for k in range(4):
@@ -125,25 +130,46 @@ def tile_memorymoco_pa_kernel(tc, x0, x1, x2, x3, mem0, mem1, mem2, mem3, out_0,
         def x_quant(v):
             nc.vector.quantize_mx(out=xc[v][:].bitcast(FP8X4), scales=xsc[v][:], in_=gxs[v][:])
 
-        def turn(t, on_scalar):
-            words = raw[t][:].bitcast(F32)
-            gs[t] = grp.tile([P, 4 * 512], BF16, name="g%d" % t, tag="g", align_bytes=64)
-            gw = gs[t][:].bitcast(F32).rearrange("k (h r q u) -> k h r q u", h=2, r=2, u=2)
-            for h in range(2):
-                pt = ptp.tile([P, 2, 2, P], F32, name="pt%d_%d" % (t, h), tag="pt")
-                for r in range(2):
-                    for u in range(2):
-                        nc.tensor.transpose(pt[:, r, u, :], words[:, 2 * h + r, u : D // 2 : 2], ident[:])
-                src = pt[:].rearrange("k r u q -> k r q u")
-                if h == 1 and on_scalar:
-                    nc.scalar.copy(out=gw[:, h], in_=src)
-                else:
-                    nc.vector.tensor_copy(out=gw[:, h], in_=src)
+        def unit(label, words, a, dest, on_scalar):
+            pt = ptp.tile([P, 4, P], F32, name="pt%s" % label, tag="pt")
+            for e in range(4):
+                nc.tensor.transpose(pt[:, e, :], words[:, 2 * a + e // 2, e % 2 : D // 2 : 2], ident[:])
+            src = pt[:].rearrange("k e p -> k p e")
+            if on_scalar:
+                nc.scalar.copy(out=dest[:, a], in_=src)
+            else:
+                nc.vector.tensor_copy(out=dest[:, a], in_=src)
 
-        def quant(t):
-            cols = slice(512 * (t % 4), 512 * (t % 4 + 1))
+        def turn0(n, on_scalar):
+            gs[n] = grp.tile([P, 4 * 512], BF16, name="g%d" % n, tag="g", align_bytes=64)
+            dest = gs[n][:].bitcast(F32).rearrange("k (p a w) -> k a p w", a=2, w=4)
+            words = raw0[n][:].bitcast(F32)
+            unit("0_%d_0" % n, words, 0, dest, False)
+            unit("0_%d_1" % n, words, 1, dest, on_scalar)
+
+        def quant0(n):
+            cols = slice(512 * n, 512 * (n + 1))
             nc.vector.quantize_mx(
-                out=mc[t // 4][:, cols].bitcast(FP8X4), scales=msc[t // 4][:, cols], in_=gs[t][:]
+                out=mc[0][:, cols].bitcast(FP8X4), scales=msc[0][:, cols], in_=gs[n][:]
+            )
+
+        def unit_w(w, on_scalar):
+            j = 1 + w // 8
+            a = w % 8
+            if a == 0:
+                gbig[j] = big.tile([P, 4 * Q], BF16, name="gb%d" % j, tag="gb", align_bytes=64)
+            dest = gbig[j][:].bitcast(F32).rearrange("k (p a w) -> k a p w", a=8, w=4)
+            unit("w%d" % w, rawj[j][:].bitcast(F32), a, dest, on_scalar)
+
+        def quant_z(z):
+            j = 1 + z // 4
+            n = z % 4
+            if n == 0:
+                new_codes(j)
+            cols = slice(512 * n, 512 * (n + 1))
+            nc.vector.quantize_mx(
+                out=mc[j][:, cols].bitcast(FP8X4), scales=msc[j][:, cols],
+                in_=gbig[j][:, 2048 * n : 2048 * (n + 1)],
             )
 
         def start_tile(c):
@@ -170,9 +196,15 @@ def tile_memorymoco_pa_kernel(tc, x0, x1, x2, x3, mem0, mem1, mem2, mem3, out_0,
                 start=True, stop=True,
             )
             nc.scalar.activation(
-                out=ot[:, m, 1 + 512 * n : 1 + 512 * (n + 1)].rearrange("b (q r) -> b q r", r=4),
-                in_=ps[:].rearrange("b (r q) -> b q r", r=4),
+                out=ot[:, m, 1 + 512 * n : 1 + 512 * (n + 1)], in_=ps[:],
                 func=ACT.Exp, scale=rs[:, k, m : m + 1],
+            )
+
+        def store_tile(c):
+            ot, o8, k = tiles[c]
+            nc.sync.dma_start(
+                out=out_0[c].rearrange("(p m) q -> p (m q)", m=2),
+                in_=ot[:].rearrange("p m q -> p (m q)"),
             )
 
         def store32(c, m, lo, hi):
@@ -195,51 +227,73 @@ def tile_memorymoco_pa_kernel(tc, x0, x1, x2, x3, mem0, mem1, mem2, mem3, out_0,
         rows_seq = [(c, m) for c in ORDER for m in range(2)]
 
         ctx.enter_context(tc.manual_schedule(engines={mybir.EngineType.DVE}))
+        new_codes(0)
         x_turn(1)
         x_turn(2)
         x_quant(1)
         x_turn(3)
         x_quant(2)
         x_quant(3)
-        turn(0, False)
+        turn0(0, False)
         scales()
-        quant(0)
+        quant0(0)
         c = ORDER[0]
         start_tile(c)
         seps = ((0, 0), (0, 1), (1, 0))
         for n in range(NCH):
-            turn(n + 1, True)
+            if n < 3:
+                turn0(n + 1, True)
             mm(c, 0, n)
             mm(c, 1, n)
             if n < 3:
                 dot(seps[n][0], seps[n][1])
-                quant(n + 1)
+                quant0(n + 1)
+            if n == 2:
+                unit_w(0, False)
+            if n == 3:
+                unit_w(1, True)
+                unit_w(2, False)
         col0(c)
-        store32(c, 0, 0, W)
-        store32(c, 1, 0, W)
+        store_tile(c)
         dot(1, 1)
-        extras = {2: ("d", 2, 0), 3: ("d", 2, 1), 4: ("x", 0), 5: ("d", 3, 0), 6: ("d", 3, 1)}
+        plan = {
+            2: ((3, 4, 5), (), ("d", 2, 0)), 3: ((6, 7), (0,), ("d", 2, 1)),
+            4: ((8,), (1, 2), ("x", 0, 0)), 5: ((9, 10), (3,), ("d", 3, 0)),
+            6: ((11, 12, 13), (), ("d", 3, 1)), 7: ((14, 15), (4,), None),
+            8: ((16,), (5, 6), None), 9: ((17, 18), (7,), None),
+            10: ((19, 20, 21), (), None), 11: ((22, 23), (8,), None),
+            12: ((), (9, 10), None), 13: ((), (11,), None),
+            14: ((), (), None), 15: ((), (), None),
+        }
         for s in range(2, 16):
             c, m = rows_seq[s]
+            units, quants, e = plan[s]
             if m == 0:
                 start_tile(c)
                 col0(c)
             if s == 2:
                 cast8(rows_seq[0][0], 0, 0, W)
-            cast8(rows_seq[s - 1][0], rows_seq[s - 1][1], 0, W)
-            t = s + 3
-            if t < 16:
-                turn(t, t % 2 == 0)
-            e = extras.get(s)
+            late_cast = len(units) == 2 and len(quants) == 1
+            if not late_cast:
+                cast8(rows_seq[s - 1][0], rows_seq[s - 1][1], 0, W)
+            for w in units:
+                unit_w(w, w % 4 == 1)
+            if late_cast:
+                cast8(rows_seq[s - 1][0], rows_seq[s - 1][1], 0, W)
             if e is not None and e[0] == "x":
                 x_turn(0)
             if e is not None and e[0] == "d":
                 dot(e[1], e[2])
-            if t - 1 < 16:
-                quant(t - 1)
+            for z in quants:
+                quant_z(z)
             if e is not None and e[0] == "x":
                 x_quant(0)
-            if s < 15:
+            if s < 14:
+                for n in range(NCH):
+                    mm(c, m, n)
+                if m == 1:
+                    store_tile(c)
+            elif s == 14:
                 for n in range(NCH):
                     mm(c, m, n)
                 store32(c, m, 0, W)

@@ -22,6 +22,7 @@ FLOPS = 2 * len(COMBOS) * B * Q * D
 P = 128
 W = Q + 1
 NCH = 4
+HALF = 1 + Q // 2
 ORDER = (3, 5, 7, 0, 6, 1, 4, 2)
 
 
@@ -32,16 +33,20 @@ def tile_memorymoco_pa_kernel(tc, x0, x1, x2, x3, mem0, mem1, mem2, mem3, out_0,
 
     with ExitStack() as ctx:
         const = ctx.enter_context(tc.tile_pool(name="const", bufs=1))
+        rawp = ctx.enter_context(tc.tile_pool(name="rawp", bufs=12))
         grp = ctx.enter_context(tc.tile_pool(name="grp", bufs=3))
-        big = ctx.enter_context(tc.tile_pool(name="big", bufs=2))
-        outp = ctx.enter_context(tc.tile_pool(name="outp", bufs=3))
+        outp = ctx.enter_context(tc.tile_pool(name="outp", bufs=4))
         ptp = ctx.enter_context(tc.psum_pool(name="ptp", bufs=3))
-        psp = ctx.enter_context(tc.psum_pool(name="psp", bufs=5))
+        psp = ctx.enter_context(tc.psum_pool(name="psp", bufs=4))
+        pdp = ctx.enter_context(tc.psum_pool(name="pdp", bufs=1))
 
         ident = const.tile([P, P], F32, name="ident")
         make_identity(nc, ident[:])
         one = const.tile([P, 1], F32, name="one")
         nc.vector.memset(one[:], 1.0)
+        zeros = const.tile([P, 512], BF16, name="zeros")
+        nc.vector.memset(zeros[:], 0.0)
+        idle = pdp.tile([P, 512], F32, name="idle")
         warm = const.tile([P, 2], F32, name="warm")
         nc.scalar.activation(out=warm[:, 0:1], in_=one[:], func=ACT.Sqrt)
 
@@ -49,17 +54,14 @@ def tile_memorymoco_pa_kernel(tc, x0, x1, x2, x3, mem0, mem1, mem2, mem3, out_0,
         for v in (1, 0, 2, 3):
             xr[v] = const.tile([P, 2, D], BF16, name="xr%d" % v)
             nc.sync.dma_start(out=xr[v][:], in_=xs[v].rearrange("(p m) k -> p m k", m=2))
-        raw0 = {}
-        for n in range(NCH):
-            raw0[n] = const.tile([P, 4, D], BF16, name="raw0_%d" % n)
+        raw = {}
+        for t in range(16):
+            raw[t] = rawp.tile([P, 4, D], BF16, name="raw%d" % t, tag="raw")
+            n = t % 4
             nc.sync.dma_start(
-                out=raw0[n][:],
-                in_=mem0[512 * n : 512 * (n + 1), :].rearrange("(p r) k -> p r k", r=4),
+                out=raw[t][:],
+                in_=mems[t // 4][512 * n : 512 * (n + 1), :].rearrange("(p r) k -> p r k", r=4),
             )
-        rawj = {}
-        for j in (1, 2, 3):
-            rawj[j] = const.tile([P, 16, D], BF16, name="rawj%d" % j)
-            nc.sync.dma_start(out=rawj[j][:], in_=mems[j].rearrange("(p r) k -> p r k", r=16))
 
         ss = const.tile([P, 8], F32, name="ss")
         nrm = const.tile([P, 8], F32, name="nrm")
@@ -81,19 +83,17 @@ def tile_memorymoco_pa_kernel(tc, x0, x1, x2, x3, mem0, mem1, mem2, mem3, out_0,
 
         xc = {}
         xsc = {}
+        mc = {}
+        msc = {}
         for v in range(4):
             xc[v] = const.tile([P, 2 * P], U32, name="xc%d" % v, align_bytes=64)
             xsc[v] = const.tile([P, 2 * P], U8, name="xsc%d" % v, align_bytes=64)
-        mc = {}
-        msc = {}
+            mc[v] = const.tile([P, Q], U32, name="mc%d" % v, align_bytes=64)
+            msc[v] = const.tile([P, Q], U8, name="msc%d" % v, align_bytes=64)
+
         gxs = {}
         gs = {}
-        gbig = {}
         tiles = {}
-
-        def new_codes(j):
-            mc[j] = big.tile([P, Q], U32, name="mc%d" % j, tag="mc", align_bytes=64)
-            msc[j] = big.tile([P, Q], U8, name="msc%d" % j, tag="msc", align_bytes=64)
 
         def scales():
             for k in range(4):
@@ -130,46 +130,25 @@ def tile_memorymoco_pa_kernel(tc, x0, x1, x2, x3, mem0, mem1, mem2, mem3, out_0,
         def x_quant(v):
             nc.vector.quantize_mx(out=xc[v][:].bitcast(FP8X4), scales=xsc[v][:], in_=gxs[v][:])
 
-        def unit(label, words, a, dest, on_scalar):
-            pt = ptp.tile([P, 4, P], F32, name="pt%s" % label, tag="pt")
-            for e in range(4):
-                nc.tensor.transpose(pt[:, e, :], words[:, 2 * a + e // 2, e % 2 : D // 2 : 2], ident[:])
-            src = pt[:].rearrange("k e p -> k p e")
-            if on_scalar:
-                nc.scalar.copy(out=dest[:, a], in_=src)
-            else:
-                nc.vector.tensor_copy(out=dest[:, a], in_=src)
+        def turn(t, on_scalar):
+            words = raw[t][:].bitcast(F32)
+            gs[t] = grp.tile([P, 4 * 512], BF16, name="g%d" % t, tag="g", align_bytes=64)
+            gw = gs[t][:].bitcast(F32).rearrange("k (h r q u) -> k h r q u", h=2, r=2, u=2)
+            for h in range(2):
+                pt = ptp.tile([P, 2, 2, P], F32, name="pt%d_%d" % (t, h), tag="pt")
+                for r in range(2):
+                    for u in range(2):
+                        nc.tensor.transpose(pt[:, r, u, :], words[:, 2 * h + r, u : D // 2 : 2], ident[:])
+                src = pt[:].rearrange("k r u q -> k r q u")
+                if h == 1 and on_scalar:
+                    nc.scalar.copy(out=gw[:, h], in_=src)
+                else:
+                    nc.vector.tensor_copy(out=gw[:, h], in_=src)
 
-        def turn0(n, on_scalar):
-            gs[n] = grp.tile([P, 4 * 512], BF16, name="g%d" % n, tag="g", align_bytes=64)
-            dest = gs[n][:].bitcast(F32).rearrange("k (p a w) -> k a p w", a=2, w=4)
-            words = raw0[n][:].bitcast(F32)
-            unit("0_%d_0" % n, words, 0, dest, False)
-            unit("0_%d_1" % n, words, 1, dest, on_scalar)
-
-        def quant0(n):
-            cols = slice(512 * n, 512 * (n + 1))
+        def quant(t):
+            cols = slice(512 * (t % 4), 512 * (t % 4 + 1))
             nc.vector.quantize_mx(
-                out=mc[0][:, cols].bitcast(FP8X4), scales=msc[0][:, cols], in_=gs[n][:]
-            )
-
-        def unit_w(w, on_scalar):
-            j = 1 + w // 8
-            a = w % 8
-            if a == 0:
-                gbig[j] = big.tile([P, 4 * Q], BF16, name="gb%d" % j, tag="gb", align_bytes=64)
-            dest = gbig[j][:].bitcast(F32).rearrange("k (p a w) -> k a p w", a=8, w=4)
-            unit("w%d" % w, rawj[j][:].bitcast(F32), a, dest, on_scalar)
-
-        def quant_z(z):
-            j = 1 + z // 4
-            n = z % 4
-            if n == 0:
-                new_codes(j)
-            cols = slice(512 * n, 512 * (n + 1))
-            nc.vector.quantize_mx(
-                out=mc[j][:, cols].bitcast(FP8X4), scales=msc[j][:, cols],
-                in_=gbig[j][:, 2048 * n : 2048 * (n + 1)],
+                out=mc[t // 4][:, cols].bitcast(FP8X4), scales=msc[t // 4][:, cols], in_=gs[t][:]
             )
 
         def start_tile(c):
@@ -196,15 +175,9 @@ def tile_memorymoco_pa_kernel(tc, x0, x1, x2, x3, mem0, mem1, mem2, mem3, out_0,
                 start=True, stop=True,
             )
             nc.scalar.activation(
-                out=ot[:, m, 1 + 512 * n : 1 + 512 * (n + 1)], in_=ps[:],
+                out=ot[:, m, 1 + 512 * n : 1 + 512 * (n + 1)].rearrange("b (q r) -> b q r", r=4),
+                in_=ps[:].rearrange("b (r q) -> b q r", r=4),
                 func=ACT.Exp, scale=rs[:, k, m : m + 1],
-            )
-
-        def store_tile(c):
-            ot, o8, k = tiles[c]
-            nc.sync.dma_start(
-                out=out_0[c].rearrange("(p m) q -> p (m q)", m=2),
-                in_=ot[:].rearrange("p m q -> p (m q)"),
             )
 
         def store32(c, m, lo, hi):
@@ -226,74 +199,68 @@ def tile_memorymoco_pa_kernel(tc, x0, x1, x2, x3, mem0, mem1, mem2, mem3, out_0,
 
         rows_seq = [(c, m) for c in ORDER for m in range(2)]
 
-        ctx.enter_context(tc.manual_schedule(engines={mybir.EngineType.DVE}))
-        new_codes(0)
+        def keep_warm(count):
+            for d in range(count):
+                nc.tensor.matmul(out=idle[:], lhsT=zeros[:, 0:P], rhs=zeros[:], start=True, stop=True)
+
+        ctx.enter_context(tc.manual_schedule(engines={mybir.EngineType.DVE, mybir.EngineType.PE}))
+        keep_warm(4)
         x_turn(1)
+        keep_warm(2)
         x_turn(2)
+        keep_warm(2)
         x_quant(1)
         x_turn(3)
+        keep_warm(2)
         x_quant(2)
         x_quant(3)
-        turn0(0, False)
+        turn(0, False)
+        keep_warm(2)
         scales()
-        quant0(0)
+        quant(0)
         c = ORDER[0]
         start_tile(c)
         seps = ((0, 0), (0, 1), (1, 0))
         for n in range(NCH):
-            if n < 3:
-                turn0(n + 1, True)
+            turn(n + 1, True)
             mm(c, 0, n)
             mm(c, 1, n)
+            keep_warm(1)
             if n < 3:
                 dot(seps[n][0], seps[n][1])
-                quant0(n + 1)
+                quant(n + 1)
+            if n == 1:
+                col0(c)
+                store32(c, 0, 0, HALF)
+                store32(c, 1, 0, HALF)
             if n == 2:
-                unit_w(0, False)
-            if n == 3:
-                unit_w(1, True)
-                unit_w(2, False)
-        col0(c)
-        store_tile(c)
+                cast8(c, 0, 0, HALF)
+                cast8(c, 1, 0, HALF)
+        store32(c, 0, HALF, W)
+        store32(c, 1, HALF, W)
         dot(1, 1)
-        plan = {
-            2: ((3, 4, 5), (), ("d", 2, 0)), 3: ((6, 7), (0,), ("d", 2, 1)),
-            4: ((8,), (1, 2), ("x", 0, 0)), 5: ((9, 10), (3,), ("d", 3, 0)),
-            6: ((11, 12, 13), (), ("d", 3, 1)), 7: ((14, 15), (4,), None),
-            8: ((16,), (5, 6), None), 9: ((17, 18), (7,), None),
-            10: ((19, 20, 21), (), None), 11: ((22, 23), (8,), None),
-            12: ((), (9, 10), None), 13: ((), (11,), None),
-            14: ((), (), None), 15: ((), (), None),
-        }
+        extras = {2: ("d", 2, 0), 3: ("d", 2, 1), 4: ("x", 0), 5: ("d", 3, 0), 6: ("d", 3, 1)}
         for s in range(2, 16):
             c, m = rows_seq[s]
-            units, quants, e = plan[s]
             if m == 0:
                 start_tile(c)
                 col0(c)
             if s == 2:
-                cast8(rows_seq[0][0], 0, 0, W)
-            late_cast = len(units) == 2 and len(quants) == 1
-            if not late_cast:
-                cast8(rows_seq[s - 1][0], rows_seq[s - 1][1], 0, W)
-            for w in units:
-                unit_w(w, w % 4 == 1)
-            if late_cast:
-                cast8(rows_seq[s - 1][0], rows_seq[s - 1][1], 0, W)
+                cast8(rows_seq[0][0], 0, HALF, W)
+            cast8(rows_seq[s - 1][0], rows_seq[s - 1][1], HALF if s == 2 else 0, W)
+            t = s + 3
+            if t < 16:
+                turn(t, t % 2 == 0)
+            e = extras.get(s)
             if e is not None and e[0] == "x":
                 x_turn(0)
             if e is not None and e[0] == "d":
                 dot(e[1], e[2])
-            for z in quants:
-                quant_z(z)
+            if t - 1 < 16:
+                quant(t - 1)
             if e is not None and e[0] == "x":
                 x_quant(0)
-            if s < 14:
-                for n in range(NCH):
-                    mm(c, m, n)
-                if m == 1:
-                    store_tile(c)
-            elif s == 14:
+            if s < 15:
                 for n in range(NCH):
                     mm(c, m, n)
                 store32(c, m, 0, W)

@@ -23,6 +23,8 @@ P = 128
 W = Q + 1
 NCH = 4
 HALF = 1 + Q // 2
+PAD = 3
+WP = PAD + W
 ORDER = (3, 5, 7, 0, 6, 1, 4, 2)
 
 
@@ -33,7 +35,6 @@ def tile_memorymoco_pa_kernel(tc, x0, x1, x2, x3, mem0, mem1, mem2, mem3, out_0,
 
     with ExitStack() as ctx:
         const = ctx.enter_context(tc.tile_pool(name="const", bufs=1))
-        rawp = ctx.enter_context(tc.tile_pool(name="rawp", bufs=12))
         grp = ctx.enter_context(tc.tile_pool(name="grp", bufs=3))
         outp = ctx.enter_context(tc.tile_pool(name="outp", bufs=4))
         ptp = ctx.enter_context(tc.psum_pool(name="ptp", bufs=3))
@@ -55,13 +56,17 @@ def tile_memorymoco_pa_kernel(tc, x0, x1, x2, x3, mem0, mem1, mem2, mem3, out_0,
             xr[v] = const.tile([P, 2, D], BF16, name="xr%d" % v)
             nc.sync.dma_start(out=xr[v][:], in_=xs[v].rearrange("(p m) k -> p m k", m=2))
         raw = {}
-        for t in range(16):
-            raw[t] = rawp.tile([P, 4, D], BF16, name="raw%d" % t, tag="raw")
-            n = t % 4
+        for n in range(4):
+            first = const.tile([P, 4, D], BF16, name="raw0_%d" % n)
             nc.sync.dma_start(
-                out=raw[t][:],
-                in_=mems[t // 4][512 * n : 512 * (n + 1), :].rearrange("(p r) k -> p r k", r=4),
+                out=first[:], in_=mems[0][512 * n : 512 * (n + 1), :].rearrange("(p r) k -> p r k", r=4)
             )
+            raw[n] = first[:].bitcast(F32)
+        for j in range(1, 4):
+            whole = const.tile([P, 16, D], BF16, name="raw%d" % j)
+            nc.sync.dma_start(out=whole[:], in_=mems[j].rearrange("(p r) k -> p r k", r=16))
+            for n in range(4):
+                raw[4 * j + n] = whole[:].bitcast(F32)[:, 4 * n : 4 * (n + 1), :]
 
         ss = const.tile([P, 8], F32, name="ss")
         nrm = const.tile([P, 8], F32, name="nrm")
@@ -131,7 +136,7 @@ def tile_memorymoco_pa_kernel(tc, x0, x1, x2, x3, mem0, mem1, mem2, mem3, out_0,
             nc.vector.quantize_mx(out=xc[v][:].bitcast(FP8X4), scales=xsc[v][:], in_=gxs[v][:])
 
         def turn(t, on_scalar):
-            words = raw[t][:].bitcast(F32)
+            words = raw[t]
             gs[t] = grp.tile([P, 4 * 512], BF16, name="g%d" % t, tag="g", align_bytes=64)
             gw = gs[t][:].bitcast(F32).rearrange("k (h r q u) -> k h r q u", h=2, r=2, u=2)
             for h in range(2):
@@ -154,13 +159,13 @@ def tile_memorymoco_pa_kernel(tc, x0, x1, x2, x3, mem0, mem1, mem2, mem3, out_0,
         def start_tile(c):
             i, j = COMBOS[c]
             k = PAIRS.index((min(i, j), max(i, j)))
-            ot = outp.tile([P, 2, W], F32, name="ot%d" % c, tag="ot")
-            o8 = outp.tile([P, 2, W], FP8, name="o8%d" % c, tag="o8")
+            ot = outp.tile([P, 2, WP], F32, name="ot%d" % c, tag="ot")
+            o8 = outp.tile([P, 2, WP], FP8, name="o8%d" % c, tag="o8")
             tiles[c] = (ot, o8, k)
 
         def col0(c):
             ot, o8, k = tiles[c]
-            nc.scalar.activation(out=ot[:, :, 0:1], in_=lg0[:, k], func=ACT.Exp)
+            nc.scalar.activation(out=ot[:, :, PAD : PAD + 1], in_=lg0[:, k], func=ACT.Exp)
 
         def mm(c, m, n):
             i, j = COMBOS[c]
@@ -174,8 +179,12 @@ def tile_memorymoco_pa_kernel(tc, x0, x1, x2, x3, mem0, mem1, mem2, mem3, out_0,
                 rhs=mc[j][:, cols].bitcast(FP8X4), rhs_scale=msc[j][:, cols],
                 start=True, stop=True,
             )
+            if j == 0:
+                dest = ot[:, m, PAD + 1 + 512 * n : PAD + 1 + 512 * (n + 1)].rearrange("b (q r) -> b q r", r=4)
+            else:
+                dest = ot[:, m, PAD + 1 : WP].rearrange("b (q s) -> b q s", s=16)[:, :, 4 * n : 4 * (n + 1)]
             nc.scalar.activation(
-                out=ot[:, m, 1 + 512 * n : 1 + 512 * (n + 1)].rearrange("b (q r) -> b q r", r=4),
+                out=dest,
                 in_=ps[:].rearrange("b (r q) -> b q r", r=4),
                 func=ACT.Exp, scale=rs[:, k, m : m + 1],
             )
@@ -183,13 +192,13 @@ def tile_memorymoco_pa_kernel(tc, x0, x1, x2, x3, mem0, mem1, mem2, mem3, out_0,
         def store32(c, m, lo, hi):
             ot, o8, k = tiles[c]
             nc.sync.dma_start(
-                out=out_0[c].rearrange("(p m) q -> p m q", m=2)[:, m, lo:hi], in_=ot[:, m, lo:hi]
+                out=out_0[c].rearrange("(p m) q -> p m q", m=2)[:, m, lo:hi], in_=ot[:, m, PAD + lo : PAD + hi]
             )
 
         def cast8(c, m, lo, hi):
             ot, o8, k = tiles[c]
             nc.vector.tensor_scalar(
-                out=o8[:, m, lo:hi], in0=ot[:, m, lo:hi], scalar1=Y_SCALE, scalar2=None,
+                out=o8[:, m, lo:hi], in0=ot[:, m, PAD + lo : PAD + hi], scalar1=Y_SCALE, scalar2=None,
                 op0=ALU.mult, saturate=False,
             )
             nc.sync.dma_start(
@@ -267,6 +276,6 @@ def tile_memorymoco_pa_kernel(tc, x0, x1, x2, x3, mem0, mem1, mem2, mem3, out_0,
             else:
                 for n in range(NCH):
                     mm(c, m, n)
-                    lo = 0 if n == 0 else 1 + 512 * n
-                    store32(c, m, lo, 1 + 512 * (n + 1))
-                    cast8(c, m, lo, 1 + 512 * (n + 1))
+                store32(c, m, 0, W)
+                cast8(c, m, 0, HALF)
+                cast8(c, m, HALF, W)

@@ -39,15 +39,11 @@ def tile_memorymoco_pa_kernel(tc, x0, x1, x2, x3, mem0, mem1, mem2, mem3, out_0,
         outp = ctx.enter_context(tc.tile_pool(name="outp", bufs=4))
         ptp = ctx.enter_context(tc.psum_pool(name="ptp", bufs=3))
         psp = ctx.enter_context(tc.psum_pool(name="psp", bufs=4))
-        pdp = ctx.enter_context(tc.psum_pool(name="pdp", bufs=1))
 
         ident = const.tile([P, P], F32, name="ident")
         make_identity(nc, ident[:])
         one = const.tile([P, 1], F32, name="one")
         nc.vector.memset(one[:], 1.0)
-        zeros = const.tile([P, 512], BF16, name="zeros")
-        nc.vector.memset(zeros[:], 0.0)
-        idle = pdp.tile([P, 512], F32, name="idle")
         warm = const.tile([P, 2], F32, name="warm")
         nc.scalar.activation(out=warm[:, 0:1], in_=one[:], func=ACT.Sqrt)
 
@@ -208,23 +204,14 @@ def tile_memorymoco_pa_kernel(tc, x0, x1, x2, x3, mem0, mem1, mem2, mem3, out_0,
 
         rows_seq = [(c, m) for c in ORDER for m in range(2)]
 
-        def keep_warm(count):
-            for d in range(count):
-                nc.tensor.matmul(out=idle[:], lhsT=zeros[:, 0:P], rhs=zeros[:], start=True, stop=True)
-
         ctx.enter_context(tc.manual_schedule(engines={mybir.EngineType.DVE, mybir.EngineType.PE}))
-        keep_warm(4)
         x_turn(1)
-        keep_warm(2)
         x_turn(2)
-        keep_warm(2)
         x_quant(1)
         x_turn(3)
-        keep_warm(2)
         x_quant(2)
         x_quant(3)
         turn(0, False)
-        keep_warm(2)
         scales()
         quant(0)
         c = ORDER[0]
@@ -234,7 +221,6 @@ def tile_memorymoco_pa_kernel(tc, x0, x1, x2, x3, mem0, mem1, mem2, mem3, out_0,
             turn(n + 1, True)
             mm(c, 0, n)
             mm(c, 1, n)
-            keep_warm(1)
             if n < 3:
                 dot(seps[n][0], seps[n][1])
                 quant(n + 1)

from contextlib import ExitStack

import concourse.mybir as mybir
from concourse.masks import make_identity

F32 = mybir.dt.float32
BF16 = mybir.dt.bfloat16
U32 = mybir.dt.uint32
U8 = mybir.dt.uint8
FP8X4 = mybir.dt.float8_e4m3fn_x4
FP8 = mybir.dt.float8_e4m3fn
ACT = mybir.ActivationFunctionType
ALU = mybir.AluOpType

B, Q, D = 256, 2048, 512
COMBOS = ((0, 1), (0, 2), (0, 3), (1, 0), (1, 2), (2, 0), (2, 1), (3, 0))
PAIRS = ((0, 1), (0, 2), (0, 3), (1, 2))
TEMP = 0.07
Y_SCALE = 140.0
FLOPS = 2 * len(COMBOS) * B * Q * D

P = 128
W = Q + 1
NCH = 4
HALF = 1 + Q // 2
PAD = 3
WP = PAD + W
ORDER = (3, 5, 7, 0, 6, 1, 4, 2)


def tile_memorymoco_pa_kernel(tc, x0, x1, x2, x3, mem0, mem1, mem2, mem3, out_0, out_1):
    nc = tc.nc
    xs = (x0, x1, x2, x3)
    mems = (mem0, mem1, mem2, mem3)

    with ExitStack() as ctx:
        const = ctx.enter_context(tc.tile_pool(name="const", bufs=1))
        grp = ctx.enter_context(tc.tile_pool(name="grp", bufs=3))
        outp = ctx.enter_context(tc.tile_pool(name="outp", bufs=4))
        ptp = ctx.enter_context(tc.psum_pool(name="ptp", bufs=3))
        psp = ctx.enter_context(tc.psum_pool(name="psp", bufs=4))

        ident = const.tile([P, P], F32, name="ident")
        make_identity(nc, ident[:])
        one = const.tile([P, 1], F32, name="one")
        nc.vector.memset(one[:], 1.0)
        warm = const.tile([P, 2], F32, name="warm")
        nc.scalar.activation(out=warm[:, 0:1], in_=one[:], func=ACT.Sqrt)

        xr = {}
        for v in (1, 0, 2, 3):
            xr[v] = const.tile([P, 2, D], BF16, name="xr%d" % v)
            nc.sync.dma_start(out=xr[v][:], in_=xs[v].rearrange("(p m) k -> p m k", m=2))
        raw = {}
        for n in range(4):
            first = const.tile([P, 4, D], BF16, name="raw0_%d" % n)
            nc.sync.dma_start(
                out=first[:], in_=mems[0][512 * n : 512 * (n + 1), :].rearrange("(p r) k -> p r k", r=4)
            )
            raw[n] = first[:].bitcast(F32)
        for j in range(1, 4):
            whole = const.tile([P, 16, D], BF16, name="raw%d" % j)
            nc.sync.dma_start(out=whole[:], in_=mems[j].rearrange("(p r) k -> p r k", r=16))
            for n in range(4):
                raw[4 * j + n] = whole[:].bitcast(F32)[:, 4 * n : 4 * (n + 1), :]

        ss = const.tile([P, 8], F32, name="ss")
        nrm = const.tile([P, 8], F32, name="nrm")
        junk_s = const.tile([P, D], BF16, name="junk_s")
        junk_v = const.tile([P, D], BF16, name="junk_v")
        for v in (1, 0, 2, 3):
            for m in range(2):
                nc.scalar.activation(
                    out=junk_s[:], in_=xr[v][:, m, :], func=ACT.Square,
                    accum_out=ss[:, 2 * v + m : 2 * v + m + 1],
                )
        nc.scalar.activation(out=nrm[:], in_=ss[:], func=ACT.Sqrt)
        nc.scalar.activation(out=warm[:, 1:2], in_=nrm[:, 0:1], func=ACT.Exp, scale=0.0)

        prod = const.tile([P, 4, 2], F32, name="prod")
        rs = const.tile([P, 4, 2], F32, name="rs")
        dots = const.tile([P, 4, 2], F32, name="dots")
        lg0 = const.tile([P, 4, 2, 1], F32, name="lg0")

        xc = {}
        xsc = {}
        mc = {}
        msc = {}
        for v in range(4):
            xc[v] = const.tile([P, 2 * P], U32, name="xc%d" % v, align_bytes=64)
            xsc[v] = const.tile([P, 2 * P], U8, name="xsc%d" % v, align_bytes=64)
            mc[v] = const.tile([P, Q], U32, name="mc%d" % v, align_bytes=64)
            msc[v] = const.tile([P, Q], U8, name="msc%d" % v, align_bytes=64)

        gxs = {}
        gs = {}
        tiles = {}

        def scales():
            for k in range(4):
                i, j = PAIRS[k]
                nc.vector.scalar_tensor_tensor(
                    out=prod[:, k, :], in0=nrm[:, 2 * i : 2 * i + 2], scalar=TEMP,
                    in1=nrm[:, 2 * j : 2 * j + 2], op0=ALU.mult, op1=ALU.mult,
                )
            nc.vector.reciprocal(out=rs[:], in_=prod[:])

        def dot(k, m):
            a, b = PAIRS[k]
            nc.vector.scalar_tensor_tensor(
                out=junk_v[:], in0=xr[a][:, m, :], scalar=1.0, in1=xr[b][:, m, :],
                op0=ALU.mult, op1=ALU.mult, accum_out=dots[:, k, m : m + 1],
            )
            if m == 1:
                nc.vector.tensor_tensor(
                    out=lg0[:, k, :, 0], in0=dots[:, k, :], in1=rs[:, k, :], op=ALU.mult
                )

        def x_turn(v):
            words = xr[v][:].bitcast(F32)
            pt = ptp.tile([P, 2, 2, P], F32, name="ptx%d" % v, tag="pt")
            for m in range(2):
                for u in range(2):
                    nc.tensor.transpose(pt[:, m, u, :], words[:, m, u : D // 2 : 2], ident[:])
            gxs[v] = grp.tile([P, 8 * P], BF16, name="gx%d" % v, tag="gx", align_bytes=64)
            nc.vector.tensor_copy(
                out=gxs[v][:].bitcast(F32).rearrange("k (m q u) -> k m q u", m=2, u=2),
                in_=pt[:].rearrange("k m u q -> k m q u"),
            )

        def x_quant(v):
            nc.vector.quantize_mx(out=xc[v][:].bitcast(FP8X4), scales=xsc[v][:], in_=gxs[v][:])

        def turn(t, on_scalar):
            words = raw[t]
            gs[t] = grp.tile([P, 4 * 512], BF16, name="g%d" % t, tag="g", align_bytes=64)
            gw = gs[t][:].bitcast(F32).rearrange("k (h r q u) -> k h r q u", h=2, r=2, u=2)
            for h in range(2):
                pt = ptp.tile([P, 2, 2, P], F32, name="pt%d_%d" % (t, h), tag="pt")
                for r in range(2):
                    for u in range(2):
                        nc.tensor.transpose(pt[:, r, u, :], words[:, 2 * h + r, u : D // 2 : 2], ident[:])
                src = pt[:].rearrange("k r u q -> k r q u")
                if h == 1 and on_scalar:
                    nc.scalar.copy(out=gw[:, h], in_=src)
                else:
                    nc.vector.tensor_copy(out=gw[:, h], in_=src)

        def quant(t):
            cols = slice(512 * (t % 4), 512 * (t % 4 + 1))
            nc.vector.quantize_mx(
                out=mc[t // 4][:, cols].bitcast(FP8X4), scales=msc[t // 4][:, cols], in_=gs[t][:]
            )

        def start_tile(c):
            i, j = COMBOS[c]
            k = PAIRS.index((min(i, j), max(i, j)))
            ot = outp.tile([P, 2, WP], F32, name="ot%d" % c, tag="ot")
            o8 = outp.tile([P, 2, WP], FP8, name="o8%d" % c, tag="o8")
            tiles[c] = (ot, o8, k)

        def col0(c):
            ot, o8, k = tiles[c]
            nc.scalar.activation(out=ot[:, :, PAD : PAD + 1], in_=lg0[:, k], func=ACT.Exp)

        def mm(c, m, n):
            i, j = COMBOS[c]
            ot, o8, k = tiles[c]
            ps = psp.tile([P, 512], F32, name="ps%d_%d_%d" % (c, m, n), tag="ps")
            rows = slice(P * m, P * (m + 1))
            cols = slice(512 * n, 512 * (n + 1))
            nc.tensor.matmul_mx(
                out=ps[:],
                lhsT=xc[i][:, rows].bitcast(FP8X4), lhsT_scale=xsc[i][:, rows],
                rhs=mc[j][:, cols].bitcast(FP8X4), rhs_scale=msc[j][:, cols],
                start=True, stop=True,
            )
            if j == 0:
                dest = ot[:, m, PAD + 1 + 512 * n : PAD + 1 + 512 * (n + 1)].rearrange("b (q r) -> b q r", r=4)
            else:
                dest = ot[:, m, PAD + 1 : WP].rearrange("b (q s) -> b q s", s=16)[:, :, 4 * n : 4 * (n + 1)]
            nc.scalar.activation(
                out=dest,
                in_=ps[:].rearrange("b (r q) -> b q r", r=4),
                func=ACT.Exp, scale=rs[:, k, m : m + 1],
            )

        def store32(c, m, lo, hi):
            ot, o8, k = tiles[c]
            nc.sync.dma_start(
                out=out_0[c].rearrange("(p m) q -> p m q", m=2)[:, m, lo:hi], in_=ot[:, m, PAD + lo : PAD + hi]
            )

        def cast8(c, m, lo, hi):
            ot, o8, k = tiles[c]
            nc.vector.tensor_scalar(
                out=o8[:, m, lo:hi], in0=ot[:, m, PAD + lo : PAD + hi], scalar1=Y_SCALE, scalar2=None,
                op0=ALU.mult, saturate=False,
            )
            nc.sync.dma_start(
                out=out_1[c].rearrange("(p m) q -> p m q", m=2)[:, m, lo:hi],
                in_=o8[:, m, lo:hi].bitcast(U8),
            )

        rows_seq = [(c, m) for c in ORDER for m in range(2)]

        ctx.enter_context(tc.manual_schedule(engines={mybir.EngineType.DVE, mybir.EngineType.PE}))
        x_turn(1)
        x_turn(2)
        x_quant(1)
        x_turn(3)
        x_quant(2)
        x_quant(3)
        turn(0, False)
        scales()
        quant(0)
        c = ORDER[0]
        start_tile(c)
        seps = ((0, 0), (0, 1), (1, 0))
        for n in range(NCH):
            turn(n + 1, True)
            mm(c, 0, n)
            mm(c, 1, n)
            if n < 3:
                dot(seps[n][0], seps[n][1])
                quant(n + 1)
            if n == 1:
                col0(c)
                store32(c, 0, 0, HALF)
                store32(c, 1, 0, HALF)
            if n == 2:
                cast8(c, 0, 0, HALF)
                cast8(c, 1, 0, HALF)
        store32(c, 0, HALF, W)
        store32(c, 1, HALF, W)
        dot(1, 1)
        extras = {2: ("d", 2, 0), 3: ("d", 2, 1), 4: ("x", 0), 5: ("d", 3, 0), 6: ("d", 3, 1)}
        for s in range(2, 16):
            c, m = rows_seq[s]
            if m == 0:
                start_tile(c)
                col0(c)
            if s == 2:
                cast8(rows_seq[0][0], 0, HALF, W)
            cast8(rows_seq[s - 1][0], rows_seq[s - 1][1], HALF if s == 2 else 0, W)
            t = s + 3
            if t < 16:
                turn(t, t % 2 == 0)
            e = extras.get(s)
            if e is not None and e[0] == "x":
                x_turn(0)
            if e is not None and e[0] == "d":
                dot(e[1], e[2])
            if t - 1 < 16:
                quant(t - 1)
            if e is not None and e[0] == "x":
                x_quant(0)
            if s < 15:
                for n in range(NCH):
                    mm(c, m, n)
                store32(c, m, 0, W)
            else:
                for n in range(NCH):
                    mm(c, m, n)
                store32(c, m, 0, W)
                cast8(c, m, 0, HALF)
                cast8(c, m, HALF, W)
